import numpy as np
import ml_dtypes


def mxq(x, axis, fmt="e4m3"):
    dtype, down = {"e4m3": (ml_dtypes.float8_e4m3fn, 7), "e5m2": (ml_dtypes.float8_e5m2, 14)}[fmt]
    v = np.moveaxis(np.asarray(x, np.float32).astype(ml_dtypes.bfloat16).astype(np.float64), axis, -1)
    blocks = v.reshape(v.shape[:-1] + (-1, 32))
    amax = np.abs(blocks).max(-1, keepdims=True)
    byte = np.maximum(np.where(amax > 0, np.frexp(amax)[1] - 1 + 127, 0) - down, 1)
    scale = np.exp2(byte - 127.0)
    codes = (blocks / scale).astype(np.float32).astype(dtype).astype(np.float64)
    return np.moveaxis((codes * scale).reshape(v.shape), -1, axis)


WIDE = False


def mx_kscale(k):
    if not WIDE:
        return np.ones(k)
    levels = np.array([10, -10, 5, -5, 0])
    if k % 512:
        return np.exp2(np.random.permutation(np.resize(levels, k // 32))).repeat(32)
    a = np.empty((k // 512, 16))
    for p in range(k // 512):
        a[p, :8] = np.random.permutation(np.resize(levels, 8))
        for g in range(8):
            far = levels[np.abs(levels - a[p, g]) >= 10]
            a[p, g + 8] = far[np.random.randint(len(far))]
    return np.exp2(a.ravel()).repeat(32)


BF16 = ml_dtypes.bfloat16


def bf(x):
    return np.asarray(x, np.float32).astype(BF16)


def f64(x):
    return np.asarray(x).astype(np.float64)


B, CIN, CK, CV, COUT, H, W, KS, DA, DB, DC = 2, 512, 512, 512, 512, 32, 64, 3, 1, 2, 4
DILS = (DA, DB, DC)
NN = KS * KS * len(DILS)
P = H * W


def rn(*shape):
    return np.random.standard_normal(shape)


def shifted(a, d, i, j):
    ap = np.pad(a, ((0, 0), (0, 0), (d, d), (d, d)))
    return ap[:, :, i * d:i * d + H, j * d:j * d + W]


def draw0():
    s, t = mx_kscale(CIN), mx_kscale(CV)
    z = 1.2 * rn(B, NN, H, W)
    e = np.exp(z - z.max(axis=1, keepdims=True))
    return {"x": bf(rn(B, CIN, H, W) * s[None, :, None, None]),
            "attn": bf(e / e.sum(axis=1, keepdims=True)),
            "v_w": bf(rn(CV, CIN) / np.sqrt(CIN) / s[None, :] * t[:, None]),
            "v_b": bf(0.2 * rn(CV) * t),
            "w_w": bf(rn(COUT, CV) * 1.5 / np.sqrt(CV) / t[None, :]),
            "w_b": bf(0.3 * rn(COUT))}


def core(x, attn, v_w, v_b, w_w, w_b):
    value = (mxq(f64(v_w), 1, "e4m3") @ mxq(f64(x).reshape(B, CIN, P), 1, "e4m3")) + f64(v_b)[None, :, None]
    vf = value.reshape(B, CV, H, W)
    a = f64(attn)
    offs = [(d, i, j) for d in DILS for i in range(KS) for j in range(KS)]
    context = sum(a[:, n:n + 1] * shifted(vf, d, i, j) for n, (d, i, j) in enumerate(offs))
    out = (mxq(f64(w_w), 1, "e4m3") @ mxq(context.reshape(B, CV, P), 1, "e4m3")) + f64(w_b)[None, :, None]
    return out.reshape(B, COUT, H, W)


def e4m3fn_bytes(y):
    return np.clip(np.asarray(y, np.float64), -448.0, 448.0).astype(np.float32).astype(ml_dtypes.float8_e4m3fn).view(np.uint8)


def e4m3fn_values(b):
    return np.asarray(b, np.uint8).view(ml_dtypes.float8_e4m3fn).astype(np.float64)


def setup_inputs():
    d = draw0()
    x0 = np.asarray(d['x']).astype(np.float64)
    s = (np.max(np.abs(x0), axis=(0, 2, 3), keepdims=True) / 448.0).astype(np.float32)
    out = {}
    for k, v in d.items():
        if k == 'x':
            out['x_bytes'] = e4m3fn_bytes(x0 / s.astype(np.float64))
            out['x_scale'] = s
        else:
            out[k] = v
    return out


def reference(x_bytes, x_scale, attn, v_w, v_b, w_w, w_b):
    return core(e4m3fn_values(x_bytes) * x_scale.astype(np.float64), attn, v_w, v_b, w_w, w_b)

@@ -1,0 +1,542 @@
+from contextlib import ExitStack
+
+import concourse.mybir as mybir
+from concourse.masks import make_identity
+
+F32 = mybir.dt.float32
+BF16 = mybir.dt.bfloat16
+U32 = mybir.dt.uint32
+U8 = mybir.dt.uint8
+FP8 = mybir.dt.float8_e4m3fn
+FP8X4 = mybir.dt.float8_e4m3fn_x4
+ALU = mybir.AluOpType
+ACT = mybir.ActivationFunctionType
+AX = mybir.AxisListType
+
+P = 128
+B, C, H, W = 2, 512, 32, 64
+DILS = (1, 2, 4)
+NPX = B * H * W
+FLOPS = 2 * NPX * C * C * 2 + 2 * 27 * NPX * C
+
+CHUNK = 8
+NCH = H // CHUNK
+KEPT_CHUNKS = (range(0, 7), range(9, 15), range(17, 23), range(25, 31))
+KEPT = tuple(r for rows in KEPT_CHUNKS for r in rows)
+LD = 196
+LONGEST = 3
+MAXSUM = 2
+SWIDEN = ((0, 2), (0, 2), (0, 1, 2, 3), (0, 1, 2, 3))
+SINTER = (1, 1, 1, 1)
+LONG = {}
+BLOCKS = (
+    (7, 8),
+    (0, 1, 2, 3, 4, 5, 6, 15, 16),
+    (9, 10, 11, 12, 13, 14, 23, 24),
+    (17, 18, 19, 20, 21, 22, 31),
+    (25, 26, 27, 28, 29, 30),
+)
+I32 = mybir.dt.int32
+DXS = (-4, -2, -1, 0, 1, 2, 4)
+
+
+def row_chains(r, longest):
+    by_dx = {}
+    for l, d in enumerate(DILS):
+        for i in range(3):
+            dy = (i - 1) * d
+            q = r + dy
+            if q < 0 or q >= H or (r in KEPT and q // CHUNK == r // CHUNK):
+                continue
+            for j in range(3):
+                dx = (j - 1) * d
+                if dy == 0 and dx == 0:
+                    if l == 0:
+                        by_dx.setdefault(0, []).append((0, 0, -1))
+                    continue
+                by_dx.setdefault(dx, []).append((dx, dy, 9 * l + 3 * i + j))
+    chains = []
+    for dx in by_dx:
+        items = by_dx[dx]
+        parts = -(-len(items) // longest)
+        size = -(-len(items) // parts)
+        for a in range(0, len(items), size):
+            chains.append(items[a : a + size])
+    return chains
+
+
+def tile_selfattentionmodulev2_pb_kernel(tc, x_bytes, x_scale, attn, v_w, v_b, w_w, w_b, out):
+    nc = tc.nc
+    with ExitStack() as ctx:
+        const = ctx.enter_context(tc.tile_pool(name="const", bufs=1))
+        stage = ctx.enter_context(tc.tile_pool(name="stage", bufs=2))
+        one = ctx.enter_context(tc.tile_pool(name="one", bufs=1))
+        vpool = ctx.enter_context(tc.tile_pool(name="vpool", bufs=19))
+        vpp = ctx.enter_context(tc.tile_pool(name="vpp", bufs=5))
+        apool = ctx.enter_context(tc.tile_pool(name="apool", bufs=18))
+        cgp = ctx.enter_context(tc.tile_pool(name="cgp", bufs=5))
+        cpool = ctx.enter_context(tc.tile_pool(name="cpool", bufs=2))
+        opool = ctx.enter_context(tc.tile_pool(name="opool", bufs=3))
+        psv = ctx.enter_context(tc.psum_pool(name="psv", bufs=4))
+        psr = ctx.enter_context(tc.psum_pool(name="psr", bufs=2))
+        psb = ctx.enter_context(tc.psum_pool(name="psb", bufs=2))
+
+        ctx.enter_context(tc.manual_schedule())
+        at = const.tile([P, 8, 160], BF16, name="at")
+        nc.vector.memset(at[:], 0.0)
+        xs = const.tile([P, 4], F32, name="xs")
+        xbs = []
+
+        def load_x(j):
+            xb = cgp.tile([P, 4, B, CHUNK * W], U8, name="xb", tag="cg", align_bytes=64)
+            xbs.append(xb)
+            for b in range(B):
+                nc.sync.dma_start(
+                    out=xbs[j][:, :, b, :],
+                    in_=x_bytes[b].rearrange("(p t) r c -> p t (r c)", t=4)[:, :, CHUNK * W * j : CHUNK * W * (j + 1)],
+                )
+
+        wv = cgp.tile([P, 4, C], BF16, name="wvraw", tag="cg", align_bytes=64)
+        nc.sync.dma_start(out=wv[:], in_=v_w.rearrange("(m t) k -> m t k", t=4))
+        for b in range(B):
+            nc.sync.dma_start(
+                out=at[0:108, :, 16 + 64 * b : 80 + 64 * b],
+                in_=attn[b].rearrange("n (q g) c -> (n q) g c", q=4),
+            )
+        nc.sync.dma_start(out=xs[:], in_=x_scale.rearrange("o (p t) a b -> p (o t a b)", t=4))
+        load_x(0)
+        load_x(1)
+        vb16 = const.tile([P, C], BF16, name="vb16")
+        nc.sync.dma_start(out=vb16[:], in_=v_b.partition_broadcast(P))
+        ww = cgp.tile([P, 4, C], BF16, name="wwraw", tag="cg", align_bytes=64)
+        nc.sync.dma_start(out=ww[:], in_=w_w.rearrange("(g o) k -> o g k", g=4))
+        wb16 = const.tile([P, P], BF16, name="wb16")
+        nc.gpsimd.memset(wb16[:], 0.0)
+        nc.sync.dma_start(out=wb16[0:4, :], in_=w_b.rearrange("(g o) -> g o", g=4))
+
+        ident = const.tile([P, P], F32, name="ident")
+        make_identity(nc, ident[:])
+        ext = const.tile([P, P + 8], F32, name="ext")
+        nc.vector.tensor_copy(out=ext[:, 4 : 4 + P], in_=ident[:])
+        nc.vector.tensor_copy(out=ext[:, 0:4], in_=ident[:, P - 4 : P])
+        nc.vector.tensor_copy(out=ext[:, P + 4 : P + 8], in_=ident[:, 0:4])
+        ident16 = const.tile([P, P], BF16, name="ident16")
+        nc.vector.tensor_copy(out=ident16[:], in_=ident[:])
+        edge = const.tile([P, 8], F32, name="edge")
+        id2 = ident[:].rearrange("p (b c) -> p b c", b=2)
+        for k, dx in enumerate(DXS):
+            if dx != 0:
+                nc.vector.tensor_reduce(
+                    out=edge[:, k : k + 1], in_=id2[:, :, max(0, dx) : W + min(0, dx)], axis=AX.XY, op=ALU.add
+                )
+
+        def make_weight(raw, nm):
+            grouped = cgp.tile([P, C, 4], BF16, name="wgrp", tag="cg", align_bytes=64)
+            for h in range(2):
+                pt = psr.tile([P, 2, 2, P], F32, name="pt", tag="row")
+                for k in range(2):
+                    words = raw[:, 2 * h + k, :].bitcast(F32)
+                    for u in range(2):
+                        nc.tensor.transpose(pt[:, k, u, :], words[:, u : 256 : 2], ident[:])
+                nc.scalar.copy(
+                    out=grouped[:, 256 * h : 256 * (h + 1), :].rearrange("p n j -> p (n j)").bitcast(F32).rearrange(
+                        "p (k r u) -> p k r u", k=2, u=2
+                    ),
+                    in_=pt[:].rearrange("p k u r -> p k r u"),
+                )
+            codes = const.tile([P, C], U32, name=nm + "c", align_bytes=64)
+            scales = const.tile([P, C], U8, name=nm + "s", align_bytes=64)
+            nc.vector.quantize_mx(
+                out=codes[:].bitcast(FP8X4), scales=scales[:], in_=grouped[:].rearrange("p n j -> p (n j)")
+            )
+            return codes, scales
+
+        vq, vqs = make_weight(wv, "vq")
+
+        wgt = const.tile([P, H, 27], F32, name="wgt")
+        dc = const.tile([P, H, 27], F32, name="dc")
+        wgt4 = wgt[:].rearrange("p (q g) n -> p q g n", q=4)
+        dc4 = dc[:].rearrange("p (q g) n -> p q g n", q=4)
+        for k, dx in sorted(enumerate(DXS), key=lambda e: abs(e[1])):
+            pa = psr.tile([P, 8, P], BF16, name="pa", tag="row")
+            for g in range(8):
+                nc.tensor.transpose(pa[:, g, :], at[:, g, 16 - dx : 144 - dx], ident16[:])
+            pv = pa[:].rearrange("p g (n q) -> p q g n", q=4)
+            if dx == 0:
+                nc.vector.tensor_copy(out=wgt4[:, :, :, 1:26:3], in_=pv[:, :, :, 1:26:3])
+                nc.vector.tensor_copy(out=dc4[:, :, :, 1:26:3], in_=pv[:, :, :, 1:26:3])
+                for k2, dx2 in enumerate(DXS):
+                    if dx2 != 0:
+                        d = abs(dx2)
+                        n0 = 9 * DILS.index(d) + dx2 // d + 1
+                        kk = DXS.index(-dx2)
+                        nc.vector.tensor_scalar(
+                            out=dc4[:, :, :, n0 : n0 + 7 : 3], in0=pv[:, :, :, n0 : n0 + 7 : 3],
+                            scalar1=edge[:, kk : kk + 1], scalar2=None, op0=ALU.mult,
+                        )
+            else:
+                d = abs(dx)
+                n0 = 9 * DILS.index(d) + dx // d + 1
+                nc.vector.tensor_scalar(
+                    out=wgt4[:, :, :, n0 : n0 + 7 : 3], in0=pv[:, :, :, n0 : n0 + 7 : 3],
+                    scalar1=edge[:, k : k + 1], scalar2=None, op0=ALU.mult,
+                )
+        wc = const.tile([P, H], F32, name="wc")
+        nc.vector.tensor_tensor(out=wc[:], in0=wgt[:, :, 4], in1=wgt[:, :, 13], op=ALU.add)
+        wc2 = const.tile([P, H], F32, name="wc2")
+        nc.vector.tensor_tensor(out=wc2[:], in0=wc[:], in1=wgt[:, :, 22], op=ALU.add)
+
+        xqs = []
+        xwide = {}
+        xgs = {}
+
+        def widen_x(j):
+            wide = one.tile([P, 4, B, CHUNK * W], BF16, name="wide", tag="wide")
+            for t in range(4):
+                src = xbs[j][:, t, :, :].rearrange("p b n -> p (b n)").bitcast(FP8)
+                dst = wide[:, t, :, :].rearrange("p b n -> p (b n)")
+                if t in SWIDEN[j]:
+                    nc.scalar.activation(out=dst, in_=src, func=ACT.Copy, scale=xs[:, t : t + 1])
+                else:
+                    nc.vector.tensor_scalar(out=dst, in0=src, scalar1=xs[:, t : t + 1], scalar2=None, op0=ALU.mult)
+            xwide[j] = wide
+
+        def interleave_x(j):
+            wide = xwide[j]
+            xg = one.tile([P, CHUNK, B, W, 4], BF16, name="xg", tag="xg", align_bytes=64)
+            for b in range(B):
+                (nc.vector.tensor_copy if b >= SINTER[j] else nc.scalar.copy)(
+                    out=xg[:, :, b, :, :], in_=wide[:, :, b, :].rearrange("p t (r c) -> p r c t", c=W)
+                )
+            xgs[j] = xg
+
+        def quantize_x(j):
+            xg = xgs[j]
+            codes = const.tile([P, CHUNK * P + 32], U32, name="xq%d" % j, align_bytes=64)
+            scales = const.tile([P, CHUNK * P + 128], U8, name="xqs%d" % j, align_bytes=64)
+            nc.gpsimd.memset(codes[:, 12:16], 0)
+            nc.gpsimd.memset(codes[:, CHUNK * P + 16 : CHUNK * P + 20], 0)
+            nc.gpsimd.memset(scales[:].bitcast(U32), 0)
+            nc.vector.quantize_mx(
+                out=codes[:, 16 : 16 + CHUNK * P].bitcast(FP8X4), scales=scales[:, 64 : 64 + CHUNK * P],
+                in_=xg[:].rearrange("p r b c t -> p (r b c t)"),
+            )
+            xqs.append((codes, scales))
+
+        vrows = {}
+        rawrow = {}
+
+        def make_vrow(r):
+            codes, scales = xqs[r // CHUNK]
+            cols = slice(16 + (r % CHUNK) * P, 16 + (r % CHUNK + 1) * P)
+            scols = slice(64 + (r % CHUNK) * P, 64 + (r % CHUNK + 1) * P)
+            pv = psv.tile([P, C], F32, name="pv", tag="v")
+            nc.tensor.matmul_mx(
+                out=pv[:], lhsT=codes[:, cols].bitcast(FP8X4), lhsT_scale=scales[:, scols],
+                rhs=vq[:].bitcast(FP8X4), rhs_scale=vqs[:], start=True, stop=True,
+            )
+            rawrow[r] = pv
+
+        def evac_vrow(r):
+            v = vpool.tile([P, C], F32, name="v", tag="v")
+            nc.vector.tensor_tensor(out=v[:], in0=rawrow[r][:], in1=vbias2, op=ALU.add)
+            vrows[r] = v
+
+        amats = {}
+        banded = {}
+        patches = {}
+
+        def make_d(y):
+            rows = KEPT_CHUNKS[y]
+            nr, r0 = len(rows), rows[0]
+            ry0 = r0 - CHUNK * y
+            dd = one.tile([P, 7 * LD + 64], F32, name="dd", tag="dd")
+            nc.gpsimd.memset(dd[:], 0.0)
+            dr = dd[:, 0 : nr * LD].rearrange("p (r l) -> p r l", l=LD)
+            for l, d in enumerate(DILS):
+                for i in (0, 2):
+                    s0 = 123 + 16 * d * (i - 1) - d
+                    nc.gpsimd.tensor_copy(
+                        out=dr[:, :, s0 : s0 + 2 * d + 1 : d], in_=dc[:, r0 : r0 + nr, 9 * l + 3 * i : 9 * l + 3 * i + 3]
+                    )
+                nc.gpsimd.tensor_copy(
+                    out=dr[:, :, 123 - d : 123 + d + 1 : 2 * d], in_=dc[:, r0 : r0 + nr, 9 * l + 3 : 9 * l + 6 : 2]
+                )
+            nc.gpsimd.tensor_copy(out=dr[:, :, 123], in_=wc2[:, r0 : r0 + nr])
+            at2 = stage.tile([P, 7, P], F32, name="at2", tag="at2")
+            for jx in range(8):
+                off = 119 - 16 * ry0 - jx
+                nc.sync.dma_start(
+                    out=at2[jx:P:8, 0:nr, :],
+                    in_=dd[jx:P:8, off : off + nr * (LD - 16)].rearrange("p (r l) -> p r l", l=LD - 16)[:, :, 0:P],
+                )
+            return at2
+
+        def make_a(y, at2):
+            nr = len(KEPT_CHUNKS[y])
+            am = stage.tile([P, 7, P], F32, name="am", tag="am")
+            for h in range(0, nr, 4):
+                n = min(4, nr - h)
+                pt = psb.tile([P, 4, P], F32, name="pta", tag="bd")
+                for k in range(n):
+                    nc.tensor.transpose(pt[:, k, :], at2[:, h + k, :], ident[:])
+                nc.scalar.copy(out=am[:, h : h + n, :], in_=pt[:, 0:n, :])
+            amats[y] = am
+
+        def make_patches(y):
+            codes, scales = xqs[y]
+            pq = stage.tile([P, 2, 8, CHUNK, 16], U32, name="pq", tag="pq", align_bytes=64)
+            ps = stage.tile([P, 2, 8, CHUNK, 16], U8, name="ps", tag="ps", align_bytes=64)
+            sw = scales[:].bitcast(I32)
+            pw = ps[:].rearrange("p a k r s -> p (a k r s)").bitcast(I32).rearrange("p (a k r s) -> p a k r s", a=2, k=8, r=8)
+            for a in range(2):
+                nc.vector.tensor_copy(
+                    out=pq[:, a].bitcast(I32),
+                    in_=codes[:, 12 + 8 * a : 12 + 8 * a + CHUNK * P].bitcast(I32).rearrange("p (r k s) -> p k r s", r=8, k=8),
+                )
+                nc.gpsimd.tensor_copy(
+                    out=pw[:, a],
+                    in_=sw[:, 15 + 2 * a : 15 + 2 * a + 256].rearrange("p (r k s) -> p k r s", r=8, k=8),
+                )
+            patches[y] = (pq, ps)
+
+        vps = {}
+        raw = {}
+
+        def pair_values(i):
+            y, k = divmod(i, 8)
+            pq, ps = patches[y]
+            pvs = []
+            for a in range(2):
+                pv = psv.tile([P, C], F32, name="pvp", tag="v")
+                nc.tensor.matmul_mx(
+                    out=pv[:], lhsT=pq[:, a, k].rearrange("p r s -> p (r s)").bitcast(FP8X4),
+                    lhsT_scale=ps[:, a, k].rearrange("p r s -> p (r s)"),
+                    rhs=vq[:].bitcast(FP8X4), rhs_scale=vqs[:], start=True, stop=True,
+                )
+                pvs.append(pv)
+            raw[i] = pvs
+
+        def pair_evac(i, a):
+            vp = vpp.tile([P, C], F32, name="vp", tag="vp")
+            nc.vector.tensor_tensor(out=vp[:], in0=raw[i][a][:], in1=vbias2, op=ALU.add)
+            vps[i, a] = vp
+
+        def pair_banded(i):
+            y, k = divmod(i, 8)
+            nr = len(KEPT_CHUNKS[y])
+            if k == 0:
+                cb = stage.tile([P, 4, 7, P], F32, name="cb", tag="cb")
+                banded[y] = cb
+            bd = psb.tile([P, 4, 7, 16], F32, name="bd", tag="bd")
+            for a in range(2):
+                big = 2 * k + a
+                for t in range(4):
+                    nc.tensor.matmul(
+                        out=bd[:, t, 0:nr, 8 * a : 8 * a + 8], lhsT=vps[i, a][:, P * t : P * (t + 1)],
+                        rhs=amats[y][:, 0:nr, 8 * big : 8 * big + 8], start=True, stop=True,
+                    )
+            nc.scalar.copy(out=banded[y][:, :, 0:nr, 16 * k : 16 * k + 16], in_=bd[:, :, 0:nr, :])
+
+        accs = {}
+
+        def row_ops(r):
+            chains = row_chains(r, LONG.get(r, LONGEST))
+            accs[r] = []
+            ops = []
+
+            def first(c):
+                dx, dy, n = c[0]
+                acc = apool.tile([P, C], F32, name="acc", tag="acc")
+                accs[r].append((dx, acc))
+                nc.scalar.activation(out=acc[:], in_=vrows[r + dy][:], func=ACT.Copy, scale=scalar_of(r, n))
+
+            def more(k, step):
+                dx, dy, n = chains[k][step]
+                acc = accs[r][k][1]
+                nc.vector.scalar_tensor_tensor(
+                    out=acc[:], in0=vrows[r + dy][:], scalar=scalar_of(r, n), in1=acc[:], op0=ALU.mult, op1=ALU.add
+                )
+
+            for c in chains:
+                ops.append(lambda c=c: first(c))
+            for step in range(1, 7):
+                for k, c in enumerate(chains):
+                    if step < len(c):
+                        ops.append(lambda k=k, step=step: more(k, step))
+            return ops
+
+        def scalar_of(r, n):
+            return wc2[:, r : r + 1] if n == -1 else wgt[:, r, n : n + 1]
+
+        banks = {}
+
+        def row_sum(r):
+            if not accs[r]:
+                return
+            bank = psr.tile([P, 4, P], F32, name="bank", tag="row")
+            todo = accs[r]
+            for t in range(4):
+                for k, (dx, acc) in enumerate(todo):
+                    nc.tensor.matmul(
+                        out=bank[:, t, :], lhsT=acc[:, P * t : P * (t + 1)], rhs=ext[:, 4 + dx : 4 + dx + P],
+                        start=(k == 0), stop=(k == len(todo) - 1), is_transpose=True,
+                    )
+            banks[r] = bank
+
+        ctxs = {}
+        have = {}
+
+        def row_out(r):
+            if r // 4 not in ctxs:
+                cg_new = cgp.tile([P, 4, P, 4], BF16, name="cg", tag="cg", align_bytes=64)
+                ctxs[r // 4] = cg_new
+            cg = ctxs[r // 4]
+            y = r // CHUNK
+            if r not in KEPT:
+                nc.scalar.copy(out=cg[:, r % 4, :, :], in_=banks[r][:].rearrange("p t n -> p n t"))
+            else:
+                side = banded[y][:, :, r - KEPT_CHUNKS[y][0], :].rearrange("p t n -> p n t")
+                if accs[r]:
+                    nc.vector.tensor_tensor(
+                        out=cg[:, r % 4, :, :], in0=banks[r][:].rearrange("p t n -> p n t"), in1=side, op=ALU.add
+                    )
+                else:
+                    nc.scalar.copy(out=cg[:, r % 4, :, :], in_=side)
+            have[r // 4] = have.get(r // 4, 0) + 1
+
+        cqs = {}
+
+        def finish_quantize(k):
+            cq = cpool.tile([P, 4 * P], U32, name="cq", tag="cq", align_bytes=64)
+            cs = cpool.tile([P, 4 * P], U8, name="cs", tag="cs", align_bytes=64)
+            nc.vector.quantize_mx(
+                out=cq[:].bitcast(FP8X4), scales=cs[:], in_=ctxs[k][:].rearrange("p r n t -> p (r n t)")
+            )
+            cqs[k] = (cq, cs)
+
+        def finish(k, gs):
+            cq, cs = cqs[k]
+            for g in gs:
+                po = psv.tile([P, 4, B, W], F32, name="po", tag="v")
+                nc.tensor.matmul_mx(
+                    out=po[:].rearrange("p r b c -> p (r b c)"),
+                    lhsT=wq[:, P * g : P * (g + 1)].bitcast(FP8X4), lhsT_scale=wqs[:, P * g : P * (g + 1)],
+                    rhs=cq[:].bitcast(FP8X4), rhs_scale=cs[:], start=True, stop=True,
+                )
+                ot = opool.tile([P, B, 4, W], F32, name="ot", tag="ot")
+                nc.scalar.activation(
+                    out=ot[:].rearrange("p b r c -> p r b c"), in_=po[:], func=ACT.Identity, bias=wbias[:, g : g + 1]
+                )
+                nc.sync.dma_start(
+                    out=out[:, P * g : P * (g + 1), 4 * k : 4 * k + 4, :].rearrange("b o r c -> o b (r c)"),
+                    in_=ot[:].rearrange("p b r c -> p b (r c)"),
+                )
+
+        widen_x(0)
+        interleave_x(0)
+        quantize_x(0)
+        at_d = {0: make_d(0)}
+        make_patches(0)
+        vbias = const.tile([P, 4, P], F32, name="vbias")
+        nc.vector.tensor_copy(out=vbias[:], in_=vb16[:].rearrange("p (m t) -> p t m", t=4))
+        vbias2 = vbias[:].rearrange("p t m -> p (t m)")
+        widen_x(1)
+        interleave_x(1)
+        quantize_x(1)
+        wq, wqs = make_weight(ww, "wq")
+        pb = psr.tile([P, P], BF16, name="pb", tag="row")
+        nc.tensor.transpose(pb[:], wb16[:], ident16[:])
+        wbias = const.tile([P, 4], F32, name="wbias")
+        nc.vector.tensor_copy(out=wbias[:], in_=pb[:, 0:4])
+        load_x(2)
+        load_x(3)
+
+        queue = []
+        for y, rows in enumerate(BLOCKS):
+            slots = 8 if y < NCH else 2
+            flat = []
+            for r in rows:
+                for f in row_ops(r):
+                    flat.append((f, None))
+                flat.append((None, r))
+            per = -(-len(flat) // slots)
+            for s in range(slots):
+                queue.append(flat[s * per : (s + 1) * per])
+        vdone = 3
+        while vdone < 13:
+            for r in range(vdone, min(13, vdone + 3)):
+                make_vrow(r)
+            for r in range(vdone, min(13, vdone + 3)):
+                evac_vrow(r)
+            vdone = min(13, vdone + 3)
+        make_a(0, at_d[0])
+        at_d[1] = make_d(1)
+        pair_values(0)
+        pair_evac(0, 0)
+        pair_evac(0, 1)
+        tosum = []
+        toq = []
+        tofin = []
+        for s in range(NCH * 8 + 9):
+            y, k = divmod(s, 8)
+            ops = queue[s] if s < len(queue) else []
+            third = -(-len(ops) // 3)
+            nxt = []
+
+            def run(part):
+                for f, r in ops[part * third : (part + 1) * third]:
+                    if f is not None:
+                        f()
+                    else:
+                        nxt.append(r)
+
+            if s < NCH * 8:
+                if k == 1 and y >= 1 and y + 1 < NCH:
+                    at_d[y + 1] = make_d(y + 1)
+                if k == 0 and y < 2:
+                    widen_x(y + 2)
+                if k == 2 and y < 2:
+                    interleave_x(y + 2)
+                if k == 3 and y < 2:
+                    quantize_x(y + 2)
+                if k == 5 and y + 1 < NCH:
+                    make_patches(y + 1)
+                if k == 7 and y + 1 < NCH:
+                    make_a(y + 1, at_d[y + 1])
+            new = []
+            if s + 1 < NCH * 8:
+                pair_values(s + 1)
+            while vdone < (min(24, 14 + max(0, s - 3)) if s < 17 else min(H, 24 + 2 * (s - 16))):
+                make_vrow(vdone)
+                new.append(vdone)
+                vdone += 1
+            fin = tofin[0:1]
+            tofin = tofin[1:]
+            for g, gs in fin:
+                finish(g, gs)
+            if s < NCH * 8:
+                pair_banded(s)
+            summed = tosum[0:MAXSUM]
+            tosum = tosum[MAXSUM:]
+            for r in summed:
+                row_sum(r)
+            run(0)
+            if s + 1 < NCH * 8:
+                pair_evac(s + 1, 0)
+            run(1)
+            if s + 1 < NCH * 8:
+                pair_evac(s + 1, 1)
+            for r in new:
+                evac_vrow(r)
+            run(2)
+            for g in toq:
+                finish_quantize(g)
+                tofin.append((g, (0, 1)))
+                tofin.append((g, (2, 3)))
+            toq = []
+            for r in summed:
+                row_out(r)
+                if have[r // 4] == 4:
+                    toq.append(r // 4)
+            tosum = tosum + nxt

@@ -25,19 +25,30 @@ KEPT_CHUNKS = (range(0, 7), range(9, 15), range(17, 23), range(25, 31))
 KEPT = tuple(r for rows in KEPT_CHUNKS for r in rows)
 LD = 196
 LONGEST = 3
+VOUT = ((4, 1), (5, 1), (5, 2), (6, 1), (6, 3), (7, 1), (7, 3))
 MAXSUM = 2
-SWIDEN = ((0, 2), (0, 2), (0, 1, 2, 3), (0, 1, 2, 3))
-SINTER = (1, 1, 1, 1)
-LONG = {}
-BLOCKS = (
-    (7, 8),
-    (0, 1, 2, 3, 4, 5, 6, 15, 16),
-    (9, 10, 11, 12, 13, 14, 23, 24),
-    (17, 18, 19, 20, 21, 22, 31),
-    (25, 26, 27, 28, 29, 30),
-)
+TAIL = 5
+SWIDEN = ((0, 2), (0, 1, 2), (0, 1, 2), (0, 1, 2, 3))
+SINTER = (1, 2, 1, 1)
+LONG = {31: 7, 9: 7, 14: 7}
+HEAVY = (7, 8, 15, 16, 23, 24, 31)
+LIGHT = ((), (4, 5, 6), (9, 10, 11, 12, 13, 14), (17, 18, 19, 20, 21, 22), (25, 26, 27))
+HSLOTS = 34
+LSLOTS = 7
+AHEAD = 3
+XAT = ((2, 1), (3, 9))
+PAT = (4, 3, 5)
+DAT = (1, 0, 0)
+LEAD = 3
+EARLY = (0, 0, 0, 0, 2)
 I32 = mybir.dt.int32
 DXS = (-4, -2, -1, 0, 1, 2, 4)
+XOUT = ((0, 12), (12, 8), (20, 8), (28, 8), (36, 8), (44, 8), (52, 12))
+GROUPS = {7: ((0,), (1, 2), (3, 4), (5,), (6,)), 6: ((0, 1), (2, 3), (4, 5), (6,))}
+SLOTS = [(y, b, g) for y, rows in enumerate(KEPT_CHUNKS) for b in range(B) for g in GROUPS[len(rows)]]
+
+
+BARE = (0, 1, 2, 3, 28, 29, 30)
 
 
 def row_chains(r, longest):
@@ -71,9 +82,10 @@ def tile_selfattentionmodulev2_pb_kernel(tc, x_bytes, x_scale, attn, v_w, v_b, w
         const = ctx.enter_context(tc.tile_pool(name="const", bufs=1))
         stage = ctx.enter_context(tc.tile_pool(name="stage", bufs=2))
         one = ctx.enter_context(tc.tile_pool(name="one", bufs=1))
-        vpool = ctx.enter_context(tc.tile_pool(name="vpool", bufs=19))
-        vpp = ctx.enter_context(tc.tile_pool(name="vpp", bufs=5))
-        apool = ctx.enter_context(tc.tile_pool(name="apool", bufs=18))
+        vpool = ctx.enter_context(tc.tile_pool(name="vpool", bufs=24))
+        vpp = ctx.enter_context(tc.tile_pool(name="vpp", bufs=6))
+        apool = ctx.enter_context(tc.tile_pool(name="apool", bufs=21))
+        big = ctx.enter_context(tc.tile_pool(name="big", bufs=3))
         cgp = ctx.enter_context(tc.tile_pool(name="cgp", bufs=5))
         cpool = ctx.enter_context(tc.tile_pool(name="cpool", bufs=2))
         opool = ctx.enter_context(tc.tile_pool(name="opool", bufs=3))
@@ -153,6 +165,44 @@ def tile_selfattentionmodulev2_pb_kernel(tc, x_bytes, x_scale, attn, v_w, v_b, w
 
         vq, vqs = make_weight(wv, "vq")
 
+        xqs = []
+        xwide = {}
+        xgs = {}
+
+        def widen_x(j):
+            wide = big.tile([P, 4, B, CHUNK * W], BF16, name="wide", tag="big", align_bytes=64)
+            for t in range(4):
+                src = xbs[j][:, t, :, :].rearrange("p b n -> p (b n)").bitcast(FP8)
+                dst = wide[:, t, :, :].rearrange("p b n -> p (b n)")
+                if t in SWIDEN[j]:
+                    nc.scalar.activation(out=dst, in_=src, func=ACT.Copy, scale=xs[:, t : t + 1])
+                else:
+                    nc.vector.tensor_scalar(out=dst, in0=src, scalar1=xs[:, t : t + 1], scalar2=None, op0=ALU.mult)
+            xwide[j] = wide
+
+        def interleave_x(j):
+            wide = xwide[j]
+            xg = big.tile([P, CHUNK, B, W, 4], BF16, name="xg", tag="big", align_bytes=64)
+            for b in range(B):
+                (nc.vector.tensor_copy if b >= SINTER[j] else nc.scalar.copy)(
+                    out=xg[:, :, b, :, :], in_=wide[:, :, b, :].rearrange("p t (r c) -> p r c t", c=W)
+                )
+            xgs[j] = xg
+
+        def quantize_x(j):
+            xg = xgs[j]
+            codes = stage.tile([P, CHUNK * P + 32], U32, name="xq", tag="xq", align_bytes=64)
+            scales = stage.tile([P, CHUNK * P + 128], U8, name="xqs", tag="xqs", align_bytes=64)
+            nc.gpsimd.memset(codes[:, CHUNK * P + 16 : CHUNK * P + 24], 0)
+            nc.gpsimd.memset(scales[:].bitcast(U32), 0)
+            nc.vector.quantize_mx(
+                out=codes[:, 16 : 16 + CHUNK * P].bitcast(FP8X4), scales=scales[:, 64 : 64 + CHUNK * P],
+                in_=xg[:].rearrange("p r b c t -> p (r b c t)"),
+            )
+            xqs.append((codes, scales))
+
+        widen_x(0)
+        interleave_x(0)
         wgt = const.tile([P, H, 27], F32, name="wgt")
         dc = const.tile([P, H, 27], F32, name="dc")
         wgt4 = wgt[:].rearrange("p (q g) n -> p q g n", q=4)
@@ -177,51 +227,14 @@ def tile_selfattentionmodulev2_pb_kernel(tc, x_bytes, x_scale, attn, v_w, v_b, w
             else:
                 d = abs(dx)
                 n0 = 9 * DILS.index(d) + dx // d + 1
-                nc.vector.tensor_scalar(
-                    out=wgt4[:, :, :, n0 : n0 + 7 : 3], in0=pv[:, :, :, n0 : n0 + 7 : 3],
-                    scalar1=edge[:, k : k + 1], scalar2=None, op0=ALU.mult,
+                nc.scalar.activation(
+                    out=wgt4[:, :, :, n0 : n0 + 7 : 3], in_=pv[:, :, :, n0 : n0 + 7 : 3],
+                    func=ACT.Copy, scale=edge[:, k : k + 1],
                 )
         wc = const.tile([P, H], F32, name="wc")
         nc.vector.tensor_tensor(out=wc[:], in0=wgt[:, :, 4], in1=wgt[:, :, 13], op=ALU.add)
         wc2 = const.tile([P, H], F32, name="wc2")
         nc.vector.tensor_tensor(out=wc2[:], in0=wc[:], in1=wgt[:, :, 22], op=ALU.add)
-
-        xqs = []
-        xwide = {}
-        xgs = {}
-
-        def widen_x(j):
-            wide = one.tile([P, 4, B, CHUNK * W], BF16, name="wide", tag="wide")
-            for t in range(4):
-                src = xbs[j][:, t, :, :].rearrange("p b n -> p (b n)").bitcast(FP8)
-                dst = wide[:, t, :, :].rearrange("p b n -> p (b n)")
-                if t in SWIDEN[j]:
-                    nc.scalar.activation(out=dst, in_=src, func=ACT.Copy, scale=xs[:, t : t + 1])
-                else:
-                    nc.vector.tensor_scalar(out=dst, in0=src, scalar1=xs[:, t : t + 1], scalar2=None, op0=ALU.mult)
-            xwide[j] = wide
-
-        def interleave_x(j):
-            wide = xwide[j]
-            xg = one.tile([P, CHUNK, B, W, 4], BF16, name="xg", tag="xg", align_bytes=64)
-            for b in range(B):
-                (nc.vector.tensor_copy if b >= SINTER[j] else nc.scalar.copy)(
-                    out=xg[:, :, b, :, :], in_=wide[:, :, b, :].rearrange("p t (r c) -> p r c t", c=W)
-                )
-            xgs[j] = xg
-
-        def quantize_x(j):
-            xg = xgs[j]
-            codes = const.tile([P, CHUNK * P + 32], U32, name="xq%d" % j, align_bytes=64)
-            scales = const.tile([P, CHUNK * P + 128], U8, name="xqs%d" % j, align_bytes=64)
-            nc.gpsimd.memset(codes[:, 12:16], 0)
-            nc.gpsimd.memset(codes[:, CHUNK * P + 16 : CHUNK * P + 20], 0)
-            nc.gpsimd.memset(scales[:].bitcast(U32), 0)
-            nc.vector.quantize_mx(
-                out=codes[:, 16 : 16 + CHUNK * P].bitcast(FP8X4), scales=scales[:, 64 : 64 + CHUNK * P],
-                in_=xg[:].rearrange("p r b c t -> p (r b c t)"),
-            )
-            xqs.append((codes, scales))
 
         vrows = {}
         rawrow = {}
@@ -264,12 +277,18 @@ def tile_selfattentionmodulev2_pb_kernel(tc, x_bytes, x_scale, attn, v_w, v_b, w
                 )
             nc.gpsimd.tensor_copy(out=dr[:, :, 123], in_=wc2[:, r0 : r0 + nr])
             at2 = stage.tile([P, 7, P], F32, name="at2", tag="at2")
-            for jx in range(8):
-                off = 119 - 16 * ry0 - jx
+            def skew(first, step, ix):
+                off = 123 - 16 * ry0 - ix
                 nc.sync.dma_start(
-                    out=at2[jx:P:8, 0:nr, :],
-                    in_=dd[jx:P:8, off : off + nr * (LD - 16)].rearrange("p (r l) -> p r l", l=LD - 16)[:, :, 0:P],
+                    out=at2[first:P:step, 0:nr, :],
+                    in_=dd[first:P:step, off : off + nr * (LD - 16)].rearrange("p (r l) -> p r l", l=LD - 16)[:, :, 0:P],
                 )
+
+            for c in range(8):
+                skew(c, 8, c if c >= 4 else c + 8)
+            for c in range(4):
+                skew(c, W, c)
+                skew(W - 4 + c, W, 12 + c)
             return at2
 
         def make_a(y, at2):
@@ -285,58 +304,100 @@ def tile_selfattentionmodulev2_pb_kernel(tc, x_bytes, x_scale, attn, v_w, v_b, w
 
         def make_patches(y):
             codes, scales = xqs[y]
-            pq = stage.tile([P, 2, 8, CHUNK, 16], U32, name="pq", tag="pq", align_bytes=64)
+            pq = big.tile([P, 2, 8, CHUNK, 16], U32, name="pq", tag="big", align_bytes=64)
             ps = stage.tile([P, 2, 8, CHUNK, 16], U8, name="ps", tag="ps", align_bytes=64)
             sw = scales[:].bitcast(I32)
             pw = ps[:].rearrange("p a k r s -> p (a k r s)").bitcast(I32).rearrange("p (a k r s) -> p a k r s", a=2, k=8, r=8)
             for a in range(2):
                 nc.vector.tensor_copy(
                     out=pq[:, a].bitcast(I32),
-                    in_=codes[:, 12 + 8 * a : 12 + 8 * a + CHUNK * P].bitcast(I32).rearrange("p (r k s) -> p k r s", r=8, k=8),
+                    in_=codes[:, 16 + 8 * a : 16 + 8 * a + CHUNK * P].bitcast(I32).rearrange("p (r k s) -> p k r s", r=8, k=8),
                 )
                 nc.gpsimd.tensor_copy(
                     out=pw[:, a],
-                    in_=sw[:, 15 + 2 * a : 15 + 2 * a + 256].rearrange("p (r k s) -> p k r s", r=8, k=8),
+                    in_=sw[:, 16 + 2 * a : 16 + 2 * a + 256].rearrange("p (r k s) -> p k r s", r=8, k=8),
                 )
             patches[y] = (pq, ps)
 
         vps = {}
         raw = {}
+        sums = {}
+        pos = {}
 
-        def pair_values(i):
-            y, k = divmod(i, 8)
+        ctxs = {}
+        have = {}
+        toq = []
+
+        def context_tile(k):
+            if k not in ctxs:
+                cg_new = cgp.tile([P, 4, P, 4], BF16, name="cg", tag="cg", align_bytes=64)
+                ctxs[k] = cg_new
+            return ctxs[k]
+
+        def group_values(s):
+            y, b, js = SLOTS[s]
             pq, ps = patches[y]
             pvs = []
-            for a in range(2):
+            for j in js:
+                k = 4 * b + j // 2
                 pv = psv.tile([P, C], F32, name="pvp", tag="v")
                 nc.tensor.matmul_mx(
-                    out=pv[:], lhsT=pq[:, a, k].rearrange("p r s -> p (r s)").bitcast(FP8X4),
-                    lhsT_scale=ps[:, a, k].rearrange("p r s -> p (r s)"),
+                    out=pv[:], lhsT=pq[:, j % 2, k].rearrange("p r s -> p (r s)").bitcast(FP8X4),
+                    lhsT_scale=ps[:, j % 2, k].rearrange("p r s -> p (r s)"),
                     rhs=vq[:].bitcast(FP8X4), rhs_scale=vqs[:], start=True, stop=True,
                 )
                 pvs.append(pv)
-            raw[i] = pvs
+            raw[s] = pvs
+            vps[s] = []
 
-        def pair_evac(i, a):
-            vp = vpp.tile([P, C], F32, name="vp", tag="vp")
-            nc.vector.tensor_tensor(out=vp[:], in0=raw[i][a][:], in1=vbias2, op=ALU.add)
-            vps[i, a] = vp
+        def group_evac(s, a):
+            if a < len(raw[s]):
+                vp = vpp.tile([P, C], F32, name="vp", tag="vp")
+                nc.vector.tensor_tensor(out=vp[:], in0=raw[s][a][:], in1=vbias2, op=ALU.add)
+                vps[s].append(vp)
 
-        def pair_banded(i):
-            y, k = divmod(i, 8)
+        def group_banded(s):
+            y, b, js = SLOTS[s]
             nr = len(KEPT_CHUNKS[y])
-            if k == 0:
+            if b == 0 and js[0] == 0:
                 cb = stage.tile([P, 4, 7, P], F32, name="cb", tag="cb")
                 banded[y] = cb
-            bd = psb.tile([P, 4, 7, 16], F32, name="bd", tag="bd")
-            for a in range(2):
-                big = 2 * k + a
+            width = sum(XOUT[j][1] for j in js)
+            bd = psb.tile([P, C], F32, name="bd", tag="bd")
+            bv = bd[:, 0 : 4 * nr * width].rearrange("p (t r c) -> p t r c", t=4, c=width)
+            at_col = 0
+            for j, vp in zip(js, vps[s]):
+                c0, w = XOUT[j]
                 for t in range(4):
                     nc.tensor.matmul(
-                        out=bd[:, t, 0:nr, 8 * a : 8 * a + 8], lhsT=vps[i, a][:, P * t : P * (t + 1)],
-                        rhs=amats[y][:, 0:nr, 8 * big : 8 * big + 8], start=True, stop=True,
+                        out=bv[:, t, :, at_col : at_col + w], lhsT=vp[:, P * t : P * (t + 1)],
+                        rhs=amats[y][:, 0:nr, W * b + c0 : W * b + c0 + w], start=True, stop=True,
                     )
-            nc.scalar.copy(out=banded[y][:, :, 0:nr, 16 * k : 16 * k + 16], in_=bd[:, :, 0:nr, :])
+                at_col += w
+            sums[s] = bv
+
+        def group_copy(s):
+            y, b, js = SLOTS[s]
+            nr = len(KEPT_CHUNKS[y])
+            c0 = W * b + XOUT[js[0]][0]
+            c1 = W * b + XOUT[js[-1]][0] + XOUT[js[-1]][1]
+            bare = [r for r in KEPT_CHUNKS[y] if r in BARE]
+            r0 = KEPT_CHUNKS[y][0]
+            if not bare:
+                nc.scalar.copy(out=banded[y][:, :, 0:nr, c0:c1], in_=sums[s])
+                return
+            lo, hi = bare[0] - r0, bare[-1] + 1 - r0
+            cg = context_tile(bare[0] // 4)
+            nc.scalar.copy(
+                out=cg[:, bare[0] % 4 : bare[-1] % 4 + 1, c0:c1, :],
+                in_=sums[s][:, :, lo:hi, :].rearrange("p t r c -> p r c t"),
+            )
+            a, b = (hi, nr) if lo == 0 else (0, lo)
+            nc.scalar.copy(out=banded[y][:, :, a:b, c0:c1], in_=sums[s][:, :, a:b, :])
+            if s + 1 == first_slot[y + 1]:
+                have[bare[0] // 4] = have.get(bare[0] // 4, 0) + len(bare)
+                if have[bare[0] // 4] == 4:
+                    toq.append(bare[0] // 4)
 
         accs = {}
 
@@ -358,13 +419,20 @@ def tile_selfattentionmodulev2_pb_kernel(tc, x_bytes, x_scale, attn, v_w, v_b, w
                     out=acc[:], in0=vrows[r + dy][:], scalar=scalar_of(r, n), in1=acc[:], op0=ALU.mult, op1=ALU.add
                 )
 
-            for c in chains:
-                ops.append(lambda c=c: first(c))
-            for step in range(1, 7):
-                for k, c in enumerate(chains):
-                    if step < len(c):
-                        ops.append(lambda k=k, step=step: more(k, step))
-            return ops
+            firsts = [(r + c[0][1], lambda c=c: first(c)) for c in chains]
+            rest = []
+            for k0 in range(0, len(chains), 2):
+                for step in range(1, 7):
+                    for k in (k0, k0 + 1):
+                        if k < len(chains) and step < len(chains[k]):
+                            rest.append((k, r + chains[k][step][1], lambda k=k, step=step: more(k, step)))
+            n = 0
+            for k, src, f in rest:
+                while n < min(len(firsts), k + LEAD):
+                    ops.append(firsts[n])
+                    n += 1
+                ops.append((src, f))
+            return ops + firsts[n:]
 
         def scalar_of(r, n):
             return wc2[:, r : r + 1] if n == -1 else wgt[:, r, n : n + 1]
@@ -384,25 +452,16 @@ def tile_selfattentionmodulev2_pb_kernel(tc, x_bytes, x_scale, attn, v_w, v_b, w
                     )
             banks[r] = bank
 
-        ctxs = {}
-        have = {}
-
         def row_out(r):
-            if r // 4 not in ctxs:
-                cg_new = cgp.tile([P, 4, P, 4], BF16, name="cg", tag="cg", align_bytes=64)
-                ctxs[r // 4] = cg_new
-            cg = ctxs[r // 4]
+            cg = context_tile(r // 4)
             y = r // CHUNK
             if r not in KEPT:
                 nc.scalar.copy(out=cg[:, r % 4, :, :], in_=banks[r][:].rearrange("p t n -> p n t"))
             else:
                 side = banded[y][:, :, r - KEPT_CHUNKS[y][0], :].rearrange("p t n -> p n t")
-                if accs[r]:
-                    nc.vector.tensor_tensor(
-                        out=cg[:, r % 4, :, :], in0=banks[r][:].rearrange("p t n -> p n t"), in1=side, op=ALU.add
-                    )
-                else:
-                    nc.scalar.copy(out=cg[:, r % 4, :, :], in_=side)
+                nc.vector.tensor_tensor(
+                    out=cg[:, r % 4, :, :], in0=banks[r][:].rearrange("p t n -> p n t"), in1=side, op=ALU.add
+                )
             have[r // 4] = have.get(r // 4, 0) + 1
 
         cqs = {}
@@ -424,118 +483,163 @@ def tile_selfattentionmodulev2_pb_kernel(tc, x_bytes, x_scale, attn, v_w, v_b, w
                     lhsT=wq[:, P * g : P * (g + 1)].bitcast(FP8X4), lhsT_scale=wqs[:, P * g : P * (g + 1)],
                     rhs=cq[:].bitcast(FP8X4), rhs_scale=cs[:], start=True, stop=True,
                 )
-                ot = opool.tile([P, B, 4, W], F32, name="ot", tag="ot")
-                nc.scalar.activation(
-                    out=ot[:].rearrange("p b r c -> p r b c"), in_=po[:], func=ACT.Identity, bias=wbias[:, g : g + 1]
-                )
+                pos[k, g] = po
+
+        def finish_store(k, gs):
+            for g in gs:
+                ot = (vpp if (k, g) in VOUT else opool).tile([P, B, 4, W], F32, name="ot", tag="vp" if (k, g) in VOUT else "ot")
+                if (k, g) in VOUT:
+                    nc.vector.tensor_scalar(
+                        out=ot[:].rearrange("p b r c -> p r b c"), in0=pos[k, g][:],
+                        scalar1=wbias[:, g : g + 1], scalar2=None, op0=ALU.add,
+                    )
+                else:
+                    nc.scalar.activation(
+                        out=ot[:].rearrange("p b r c -> p r b c"), in_=pos[k, g][:], func=ACT.Identity,
+                        bias=wbias[:, g : g + 1],
+                    )
                 nc.sync.dma_start(
                     out=out[:, P * g : P * (g + 1), 4 * k : 4 * k + 4, :].rearrange("b o r c -> o b (r c)"),
                     in_=ot[:].rearrange("p b r c -> p b (r c)"),
                 )
 
-        widen_x(0)
-        interleave_x(0)
         quantize_x(0)
         at_d = {0: make_d(0)}
         make_patches(0)
+        widen_x(1)
         vbias = const.tile([P, 4, P], F32, name="vbias")
         nc.vector.tensor_copy(out=vbias[:], in_=vb16[:].rearrange("p (m t) -> p t m", t=4))
         vbias2 = vbias[:].rearrange("p t m -> p (t m)")
-        widen_x(1)
+        make_vrow(3)
+        make_vrow(4)
+        make_vrow(5)
         interleave_x(1)
+        for r in (3, 4, 5):
+            evac_vrow(r)
+        make_vrow(6)
+        make_vrow(7)
+        evac_vrow(6)
+        evac_vrow(7)
         quantize_x(1)
         wq, wqs = make_weight(ww, "wq")
+        load_x(2)
+        load_x(3)
+        first_slot = [min(s for s in range(len(SLOTS)) if SLOTS[s][0] == y) for y in range(NCH)] + [len(SLOTS)]
+
+        def flatten(rows):
+            flat = []
+            for r in rows:
+                for src, f in row_ops(r):
+                    flat.append((f, r, src))
+                flat.append((None, r, 0))
+            return flat
+
+        heavy = flatten(HEAVY)
+        light = [flatten(rows) for rows in LIGHT]
+        queue = []
+        for s in range(len(SLOTS) + 4):
+            here = [heavy[len(heavy) * s // HSLOTS : len(heavy) * (s + 1) // HSLOTS]]
+            for y in range(NCH + 1):
+                k = s - first_slot[y] + EARLY[y]
+                n = LSLOTS if y < NCH else TAIL
+                if 0 <= k < n:
+                    here.append(light[y][len(light[y]) * k // n : len(light[y]) * (k + 1) // n])
+            mixed = []
+            for m in range(max(len(h) for h in here)):
+                mixed += [h[m] for h in here if m < len(h)]
+            queue.append(mixed)
+        upto = [max([12] + [src for q in queue[: s + 1 + AHEAD] for f, r, src in q]) for s in range(len(queue))]
+        for r in range(8, 11):
+            make_vrow(r)
+        for r in range(8, 11):
+            evac_vrow(r)
+        make_a(0, at_d[0])
+        at_d[1] = make_d(1)
+        for s in range(2):
+            group_values(s)
+            group_evac(s, 0)
+            group_evac(s, 1)
+        for r in range(11, 13):
+            make_vrow(r)
+            evac_vrow(r)
+        vdone = 13
         pb = psr.tile([P, P], BF16, name="pb", tag="row")
         nc.tensor.transpose(pb[:], wb16[:], ident16[:])
         wbias = const.tile([P, 4], F32, name="wbias")
         nc.vector.tensor_copy(out=wbias[:], in_=pb[:, 0:4])
-        load_x(2)
-        load_x(3)
-
-        queue = []
-        for y, rows in enumerate(BLOCKS):
-            slots = 8 if y < NCH else 2
-            flat = []
-            for r in rows:
-                for f in row_ops(r):
-                    flat.append((f, None))
-                flat.append((None, r))
-            per = -(-len(flat) // slots)
-            for s in range(slots):
-                queue.append(flat[s * per : (s + 1) * per])
-        vdone = 3
-        while vdone < 13:
-            for r in range(vdone, min(13, vdone + 3)):
-                make_vrow(r)
-            for r in range(vdone, min(13, vdone + 3)):
-                evac_vrow(r)
-            vdone = min(13, vdone + 3)
-        make_a(0, at_d[0])
-        at_d[1] = make_d(1)
-        pair_values(0)
-        pair_evac(0, 0)
-        pair_evac(0, 1)
         tosum = []
-        toq = []
+        summed = []
         tofin = []
-        for s in range(NCH * 8 + 9):
-            y, k = divmod(s, 8)
+        n_slots = len(SLOTS)
+        ready = []
+        for s in range(n_slots + 12):
+            y = SLOTS[s][0] if s < n_slots else NCH
+            k = s - first_slot[y]
             ops = queue[s] if s < len(queue) else []
             third = -(-len(ops) // 3)
             nxt = []
 
             def run(part):
-                for f, r in ops[part * third : (part + 1) * third]:
+                for f, r, src in ops[part * third : (part + 1) * third]:
                     if f is not None:
                         f()
                     else:
                         nxt.append(r)
 
-            if s < NCH * 8:
-                if k == 1 and y >= 1 and y + 1 < NCH:
+            if s < n_slots:
+                if y >= 1 and y + 1 < NCH and k == DAT[y]:
                     at_d[y + 1] = make_d(y + 1)
-                if k == 0 and y < 2:
-                    widen_x(y + 2)
-                if k == 2 and y < 2:
-                    interleave_x(y + 2)
-                if k == 3 and y < 2:
-                    quantize_x(y + 2)
-                if k == 5 and y + 1 < NCH:
+                for j, at_slot in XAT:
+                    if s == at_slot:
+                        widen_x(j)
+                    if s == at_slot + 1:
+                        interleave_x(j)
+                    if s == at_slot + 2:
+                        quantize_x(j)
+                if y + 1 < NCH and k == PAT[y]:
                     make_patches(y + 1)
-                if k == 7 and y + 1 < NCH:
+                if y + 1 < NCH and k == PAT[y] + 1:
                     make_a(y + 1, at_d[y + 1])
             new = []
-            if s + 1 < NCH * 8:
-                pair_values(s + 1)
-            while vdone < (min(24, 14 + max(0, s - 3)) if s < 17 else min(H, 24 + 2 * (s - 16))):
+            if s + 2 < n_slots:
+                group_values(s + 2)
+            while s < n_slots and vdone <= upto[s]:
                 make_vrow(vdone)
                 new.append(vdone)
                 vdone += 1
-            fin = tofin[0:1]
-            tofin = tofin[1:]
+            n_fin = 1 if s < n_slots else 2
+            fin = ready[0:n_fin]
+            ready = ready[n_fin:] + tofin
+            tofin = []
             for g, gs in fin:
                 finish(g, gs)
-            if s < NCH * 8:
-                pair_banded(s)
+            if s < n_slots:
+                group_banded(s)
+            outs = summed
             summed = tosum[0:MAXSUM]
             tosum = tosum[MAXSUM:]
             for r in summed:
                 row_sum(r)
             run(0)
-            if s + 1 < NCH * 8:
-                pair_evac(s + 1, 0)
+            if s + 2 < n_slots:
+                group_evac(s + 2, 0)
             run(1)
-            if s + 1 < NCH * 8:
-                pair_evac(s + 1, 1)
+            if s + 2 < n_slots:
+                group_evac(s + 2, 1)
             for r in new:
                 evac_vrow(r)
             run(2)
-            for g in toq:
+            for g, gs in fin:
+                finish_store(g, gs)
+            if s < n_slots:
+                group_copy(s)
+            now = [g for g in toq]
+            toq.clear()
+            for g in now:
                 finish_quantize(g)
                 tofin.append((g, (0, 1)))
                 tofin.append((g, (2, 3)))
-            toq = []
-            for r in summed:
+            for r in outs:
                 row_out(r)
                 if have[r // 4] == 4:
                     toq.append(r // 4)

from contextlib import ExitStack

import concourse.mybir as mybir
from concourse.masks import make_identity

F32 = mybir.dt.float32
BF16 = mybir.dt.bfloat16
U32 = mybir.dt.uint32
U8 = mybir.dt.uint8
FP8 = mybir.dt.float8_e4m3fn
FP8X4 = mybir.dt.float8_e4m3fn_x4
ALU = mybir.AluOpType
ACT = mybir.ActivationFunctionType
AX = mybir.AxisListType

P = 128
B, C, H, W = 2, 512, 32, 64
DILS = (1, 2, 4)
NPX = B * H * W
FLOPS = 2 * NPX * C * C * 2 + 2 * 27 * NPX * C

CHUNK = 8
NCH = H // CHUNK
KEPT_CHUNKS = (range(0, 7), range(9, 15), range(17, 23), range(25, 31))
KEPT = tuple(r for rows in KEPT_CHUNKS for r in rows)
LD = 196
LONGEST = 3
VOUT = ((4, 1), (5, 1), (5, 2), (6, 1), (6, 3), (7, 1), (7, 3))
MAXSUM = 2
TAIL = 5
SWIDEN = ((0, 2), (0, 1, 2), (0, 1, 2), (0, 1, 2, 3))
SINTER = (1, 2, 1, 1)
LONG = {31: 7, 9: 7, 14: 7}
HEAVY = (7, 8, 15, 16, 23, 24, 31)
LIGHT = ((), (4, 5, 6), (9, 10, 11, 12, 13, 14), (17, 18, 19, 20, 21, 22), (25, 26, 27))
HSLOTS = 34
LSLOTS = 7
AHEAD = 3
XAT = ((2, 1), (3, 9))
PAT = (4, 3, 5)
DAT = (1, 0, 0)
LEAD = 3
EARLY = (0, 0, 0, 0, 2)
I32 = mybir.dt.int32
DXS = (-4, -2, -1, 0, 1, 2, 4)
XOUT = ((0, 12), (12, 8), (20, 8), (28, 8), (36, 8), (44, 8), (52, 12))
GROUPS = {7: ((0,), (1, 2), (3, 4), (5,), (6,)), 6: ((0, 1), (2, 3), (4, 5), (6,))}
SLOTS = [(y, b, g) for y, rows in enumerate(KEPT_CHUNKS) for b in range(B) for g in GROUPS[len(rows)]]


BARE = (0, 1, 2, 3, 28, 29, 30)


def row_chains(r, longest):
    by_dx = {}
    for l, d in enumerate(DILS):
        for i in range(3):
            dy = (i - 1) * d
            q = r + dy
            if q < 0 or q >= H or (r in KEPT and q // CHUNK == r // CHUNK):
                continue
            for j in range(3):
                dx = (j - 1) * d
                if dy == 0 and dx == 0:
                    if l == 0:
                        by_dx.setdefault(0, []).append((0, 0, -1))
                    continue
                by_dx.setdefault(dx, []).append((dx, dy, 9 * l + 3 * i + j))
    chains = []
    for dx in by_dx:
        items = by_dx[dx]
        parts = -(-len(items) // longest)
        size = -(-len(items) // parts)
        for a in range(0, len(items), size):
            chains.append(items[a : a + size])
    return chains


def tile_selfattentionmodulev2_pb_kernel(tc, x_bytes, x_scale, attn, v_w, v_b, w_w, w_b, out):
    nc = tc.nc
    with ExitStack() as ctx:
        const = ctx.enter_context(tc.tile_pool(name="const", bufs=1))
        stage = ctx.enter_context(tc.tile_pool(name="stage", bufs=2))
        one = ctx.enter_context(tc.tile_pool(name="one", bufs=1))
        vpool = ctx.enter_context(tc.tile_pool(name="vpool", bufs=24))
        vpp = ctx.enter_context(tc.tile_pool(name="vpp", bufs=6))
        apool = ctx.enter_context(tc.tile_pool(name="apool", bufs=21))
        big = ctx.enter_context(tc.tile_pool(name="big", bufs=3))
        cgp = ctx.enter_context(tc.tile_pool(name="cgp", bufs=5))
        cpool = ctx.enter_context(tc.tile_pool(name="cpool", bufs=2))
        opool = ctx.enter_context(tc.tile_pool(name="opool", bufs=3))
        psv = ctx.enter_context(tc.psum_pool(name="psv", bufs=4))
        psr = ctx.enter_context(tc.psum_pool(name="psr", bufs=2))
        psb = ctx.enter_context(tc.psum_pool(name="psb", bufs=2))

        ctx.enter_context(tc.manual_schedule())
        at = const.tile([P, 8, 160], BF16, name="at")
        nc.vector.memset(at[:], 0.0)
        xs = const.tile([P, 4], F32, name="xs")
        xbs = []

        def load_x(j):
            xb = cgp.tile([P, 4, B, CHUNK * W], U8, name="xb", tag="cg", align_bytes=64)
            xbs.append(xb)
            for b in range(B):
                nc.sync.dma_start(
                    out=xbs[j][:, :, b, :],
                    in_=x_bytes[b].rearrange("(p t) r c -> p t (r c)", t=4)[:, :, CHUNK * W * j : CHUNK * W * (j + 1)],
                )

        wv = cgp.tile([P, 4, C], BF16, name="wvraw", tag="cg", align_bytes=64)
        nc.sync.dma_start(out=wv[:], in_=v_w.rearrange("(m t) k -> m t k", t=4))
        for b in range(B):
            nc.sync.dma_start(
                out=at[0:108, :, 16 + 64 * b : 80 + 64 * b],
                in_=attn[b].rearrange("n (q g) c -> (n q) g c", q=4),
            )
        nc.sync.dma_start(out=xs[:], in_=x_scale.rearrange("o (p t) a b -> p (o t a b)", t=4))
        load_x(0)
        load_x(1)
        vb16 = const.tile([P, C], BF16, name="vb16")
        nc.sync.dma_start(out=vb16[:], in_=v_b.partition_broadcast(P))
        ww = cgp.tile([P, 4, C], BF16, name="wwraw", tag="cg", align_bytes=64)
        nc.sync.dma_start(out=ww[:], in_=w_w.rearrange("(g o) k -> o g k", g=4))
        wb16 = const.tile([P, P], BF16, name="wb16")
        nc.gpsimd.memset(wb16[:], 0.0)
        nc.sync.dma_start(out=wb16[0:4, :], in_=w_b.rearrange("(g o) -> g o", g=4))

        ident = const.tile([P, P], F32, name="ident")
        make_identity(nc, ident[:])
        ext = const.tile([P, P + 8], F32, name="ext")
        nc.vector.tensor_copy(out=ext[:, 4 : 4 + P], in_=ident[:])
        nc.vector.tensor_copy(out=ext[:, 0:4], in_=ident[:, P - 4 : P])
        nc.vector.tensor_copy(out=ext[:, P + 4 : P + 8], in_=ident[:, 0:4])
        ident16 = const.tile([P, P], BF16, name="ident16")
        nc.vector.tensor_copy(out=ident16[:], in_=ident[:])
        edge = const.tile([P, 8], F32, name="edge")
        id2 = ident[:].rearrange("p (b c) -> p b c", b=2)
        for k, dx in enumerate(DXS):
            if dx != 0:
                nc.vector.tensor_reduce(
                    out=edge[:, k : k + 1], in_=id2[:, :, max(0, dx) : W + min(0, dx)], axis=AX.XY, op=ALU.add
                )

        def make_weight(raw, nm):
            grouped = cgp.tile([P, C, 4], BF16, name="wgrp", tag="cg", align_bytes=64)
            for h in range(2):
                pt = psr.tile([P, 2, 2, P], F32, name="pt", tag="row")
                for k in range(2):
                    words = raw[:, 2 * h + k, :].bitcast(F32)
                    for u in range(2):
                        nc.tensor.transpose(pt[:, k, u, :], words[:, u : 256 : 2], ident[:])
                nc.scalar.copy(
                    out=grouped[:, 256 * h : 256 * (h + 1), :].rearrange("p n j -> p (n j)").bitcast(F32).rearrange(
                        "p (k r u) -> p k r u", k=2, u=2
                    ),
                    in_=pt[:].rearrange("p k u r -> p k r u"),
                )
            codes = const.tile([P, C], U32, name=nm + "c", align_bytes=64)
            scales = const.tile([P, C], U8, name=nm + "s", align_bytes=64)
            nc.vector.quantize_mx(
                out=codes[:].bitcast(FP8X4), scales=scales[:], in_=grouped[:].rearrange("p n j -> p (n j)")
            )
            return codes, scales

        vq, vqs = make_weight(wv, "vq")

        xqs = []
        xwide = {}
        xgs = {}

        def widen_x(j):
            wide = big.tile([P, 4, B, CHUNK * W], BF16, name="wide", tag="big", align_bytes=64)
            for t in range(4):
                src = xbs[j][:, t, :, :].rearrange("p b n -> p (b n)").bitcast(FP8)
                dst = wide[:, t, :, :].rearrange("p b n -> p (b n)")
                if t in SWIDEN[j]:
                    nc.scalar.activation(out=dst, in_=src, func=ACT.Copy, scale=xs[:, t : t + 1])
                else:
                    nc.vector.tensor_scalar(out=dst, in0=src, scalar1=xs[:, t : t + 1], scalar2=None, op0=ALU.mult)
            xwide[j] = wide

        def interleave_x(j):
            wide = xwide[j]
            xg = big.tile([P, CHUNK, B, W, 4], BF16, name="xg", tag="big", align_bytes=64)
            for b in range(B):
                (nc.vector.tensor_copy if b >= SINTER[j] else nc.scalar.copy)(
                    out=xg[:, :, b, :, :], in_=wide[:, :, b, :].rearrange("p t (r c) -> p r c t", c=W)
                )
            xgs[j] = xg

        def quantize_x(j):
            xg = xgs[j]
            codes = stage.tile([P, CHUNK * P + 32], U32, name="xq", tag="xq", align_bytes=64)
            scales = stage.tile([P, CHUNK * P + 128], U8, name="xqs", tag="xqs", align_bytes=64)
            nc.gpsimd.memset(codes[:, CHUNK * P + 16 : CHUNK * P + 24], 0)
            nc.gpsimd.memset(scales[:].bitcast(U32), 0)
            nc.vector.quantize_mx(
                out=codes[:, 16 : 16 + CHUNK * P].bitcast(FP8X4), scales=scales[:, 64 : 64 + CHUNK * P],
                in_=xg[:].rearrange("p r b c t -> p (r b c t)"),
            )
            xqs.append((codes, scales))

        widen_x(0)
        interleave_x(0)
        wgt = const.tile([P, H, 27], F32, name="wgt")
        dc = const.tile([P, H, 27], F32, name="dc")
        wgt4 = wgt[:].rearrange("p (q g) n -> p q g n", q=4)
        dc4 = dc[:].rearrange("p (q g) n -> p q g n", q=4)
        for k, dx in sorted(enumerate(DXS), key=lambda e: abs(e[1])):
            pa = psr.tile([P, 8, P], BF16, name="pa", tag="row")
            for g in range(8):
                nc.tensor.transpose(pa[:, g, :], at[:, g, 16 - dx : 144 - dx], ident16[:])
            pv = pa[:].rearrange("p g (n q) -> p q g n", q=4)
            if dx == 0:
                nc.vector.tensor_copy(out=wgt4[:, :, :, 1:26:3], in_=pv[:, :, :, 1:26:3])
                nc.vector.tensor_copy(out=dc4[:, :, :, 1:26:3], in_=pv[:, :, :, 1:26:3])
                for k2, dx2 in enumerate(DXS):
                    if dx2 != 0:
                        d = abs(dx2)
                        n0 = 9 * DILS.index(d) + dx2 // d + 1
                        kk = DXS.index(-dx2)
                        nc.vector.tensor_scalar(
                            out=dc4[:, :, :, n0 : n0 + 7 : 3], in0=pv[:, :, :, n0 : n0 + 7 : 3],
                            scalar1=edge[:, kk : kk + 1], scalar2=None, op0=ALU.mult,
                        )
            else:
                d = abs(dx)
                n0 = 9 * DILS.index(d) + dx // d + 1
                nc.scalar.activation(
                    out=wgt4[:, :, :, n0 : n0 + 7 : 3], in_=pv[:, :, :, n0 : n0 + 7 : 3],
                    func=ACT.Copy, scale=edge[:, k : k + 1],
                )
        wc = const.tile([P, H], F32, name="wc")
        nc.vector.tensor_tensor(out=wc[:], in0=wgt[:, :, 4], in1=wgt[:, :, 13], op=ALU.add)
        wc2 = const.tile([P, H], F32, name="wc2")
        nc.vector.tensor_tensor(out=wc2[:], in0=wc[:], in1=wgt[:, :, 22], op=ALU.add)

        vrows = {}
        rawrow = {}

        def make_vrow(r):
            codes, scales = xqs[r // CHUNK]
            cols = slice(16 + (r % CHUNK) * P, 16 + (r % CHUNK + 1) * P)
            scols = slice(64 + (r % CHUNK) * P, 64 + (r % CHUNK + 1) * P)
            pv = psv.tile([P, C], F32, name="pv", tag="v")
            nc.tensor.matmul_mx(
                out=pv[:], lhsT=codes[:, cols].bitcast(FP8X4), lhsT_scale=scales[:, scols],
                rhs=vq[:].bitcast(FP8X4), rhs_scale=vqs[:], start=True, stop=True,
            )
            rawrow[r] = pv

        def evac_vrow(r):
            v = vpool.tile([P, C], F32, name="v", tag="v")
            nc.vector.tensor_tensor(out=v[:], in0=rawrow[r][:], in1=vbias2, op=ALU.add)
            vrows[r] = v

        amats = {}
        banded = {}
        patches = {}

        def make_d(y):
            rows = KEPT_CHUNKS[y]
            nr, r0 = len(rows), rows[0]
            ry0 = r0 - CHUNK * y
            dd = one.tile([P, 7 * LD + 64], F32, name="dd", tag="dd")
            nc.gpsimd.memset(dd[:], 0.0)
            dr = dd[:, 0 : nr * LD].rearrange("p (r l) -> p r l", l=LD)
            for l, d in enumerate(DILS):
                for i in (0, 2):
                    s0 = 123 + 16 * d * (i - 1) - d
                    nc.gpsimd.tensor_copy(
                        out=dr[:, :, s0 : s0 + 2 * d + 1 : d], in_=dc[:, r0 : r0 + nr, 9 * l + 3 * i : 9 * l + 3 * i + 3]
                    )
                nc.gpsimd.tensor_copy(
                    out=dr[:, :, 123 - d : 123 + d + 1 : 2 * d], in_=dc[:, r0 : r0 + nr, 9 * l + 3 : 9 * l + 6 : 2]
                )
            nc.gpsimd.tensor_copy(out=dr[:, :, 123], in_=wc2[:, r0 : r0 + nr])
            at2 = stage.tile([P, 7, P], F32, name="at2", tag="at2")
            def skew(first, step, ix):
                off = 123 - 16 * ry0 - ix
                nc.sync.dma_start(
                    out=at2[first:P:step, 0:nr, :],
                    in_=dd[first:P:step, off : off + nr * (LD - 16)].rearrange("p (r l) -> p r l", l=LD - 16)[:, :, 0:P],
                )

            for c in range(8):
                skew(c, 8, c if c >= 4 else c + 8)
            for c in range(4):
                skew(c, W, c)
                skew(W - 4 + c, W, 12 + c)
            return at2

        def make_a(y, at2):
            nr = len(KEPT_CHUNKS[y])
            am = stage.tile([P, 7, P], F32, name="am", tag="am")
            for h in range(0, nr, 4):
                n = min(4, nr - h)
                pt = psb.tile([P, 4, P], F32, name="pta", tag="bd")
                for k in range(n):
                    nc.tensor.transpose(pt[:, k, :], at2[:, h + k, :], ident[:])
                nc.scalar.copy(out=am[:, h : h + n, :], in_=pt[:, 0:n, :])
            amats[y] = am

        def make_patches(y):
            codes, scales = xqs[y]
            pq = big.tile([P, 2, 8, CHUNK, 16], U32, name="pq", tag="big", align_bytes=64)
            ps = stage.tile([P, 2, 8, CHUNK, 16], U8, name="ps", tag="ps", align_bytes=64)
            sw = scales[:].bitcast(I32)
            pw = ps[:].rearrange("p a k r s -> p (a k r s)").bitcast(I32).rearrange("p (a k r s) -> p a k r s", a=2, k=8, r=8)
            for a in range(2):
                nc.vector.tensor_copy(
                    out=pq[:, a].bitcast(I32),
                    in_=codes[:, 16 + 8 * a : 16 + 8 * a + CHUNK * P].bitcast(I32).rearrange("p (r k s) -> p k r s", r=8, k=8),
                )
                nc.gpsimd.tensor_copy(
                    out=pw[:, a],
                    in_=sw[:, 16 + 2 * a : 16 + 2 * a + 256].rearrange("p (r k s) -> p k r s", r=8, k=8),
                )
            patches[y] = (pq, ps)

        vps = {}
        raw = {}
        sums = {}
        pos = {}

        ctxs = {}
        have = {}
        toq = []

        def context_tile(k):
            if k not in ctxs:
                cg_new = cgp.tile([P, 4, P, 4], BF16, name="cg", tag="cg", align_bytes=64)
                ctxs[k] = cg_new
            return ctxs[k]

        def group_values(s):
            y, b, js = SLOTS[s]
            pq, ps = patches[y]
            pvs = []
            for j in js:
                k = 4 * b + j // 2
                pv = psv.tile([P, C], F32, name="pvp", tag="v")
                nc.tensor.matmul_mx(
                    out=pv[:], lhsT=pq[:, j % 2, k].rearrange("p r s -> p (r s)").bitcast(FP8X4),
                    lhsT_scale=ps[:, j % 2, k].rearrange("p r s -> p (r s)"),
                    rhs=vq[:].bitcast(FP8X4), rhs_scale=vqs[:], start=True, stop=True,
                )
                pvs.append(pv)
            raw[s] = pvs
            vps[s] = []

        def group_evac(s, a):
            if a < len(raw[s]):
                vp = vpp.tile([P, C], F32, name="vp", tag="vp")
                nc.vector.tensor_tensor(out=vp[:], in0=raw[s][a][:], in1=vbias2, op=ALU.add)
                vps[s].append(vp)

        def group_banded(s):
            y, b, js = SLOTS[s]
            nr = len(KEPT_CHUNKS[y])
            if b == 0 and js[0] == 0:
                cb = stage.tile([P, 4, 7, P], F32, name="cb", tag="cb")
                banded[y] = cb
            width = sum(XOUT[j][1] for j in js)
            bd = psb.tile([P, C], F32, name="bd", tag="bd")
            bv = bd[:, 0 : 4 * nr * width].rearrange("p (t r c) -> p t r c", t=4, c=width)
            at_col = 0
            for j, vp in zip(js, vps[s]):
                c0, w = XOUT[j]
                for t in range(4):
                    nc.tensor.matmul(
                        out=bv[:, t, :, at_col : at_col + w], lhsT=vp[:, P * t : P * (t + 1)],
                        rhs=amats[y][:, 0:nr, W * b + c0 : W * b + c0 + w], start=True, stop=True,
                    )
                at_col += w
            sums[s] = bv

        def group_copy(s):
            y, b, js = SLOTS[s]
            nr = len(KEPT_CHUNKS[y])
            c0 = W * b + XOUT[js[0]][0]
            c1 = W * b + XOUT[js[-1]][0] + XOUT[js[-1]][1]
            bare = [r for r in KEPT_CHUNKS[y] if r in BARE]
            r0 = KEPT_CHUNKS[y][0]
            if not bare:
                nc.scalar.copy(out=banded[y][:, :, 0:nr, c0:c1], in_=sums[s])
                return
            lo, hi = bare[0] - r0, bare[-1] + 1 - r0
            cg = context_tile(bare[0] // 4)
            nc.scalar.copy(
                out=cg[:, bare[0] % 4 : bare[-1] % 4 + 1, c0:c1, :],
                in_=sums[s][:, :, lo:hi, :].rearrange("p t r c -> p r c t"),
            )
            a, b = (hi, nr) if lo == 0 else (0, lo)
            nc.scalar.copy(out=banded[y][:, :, a:b, c0:c1], in_=sums[s][:, :, a:b, :])
            if s + 1 == first_slot[y + 1]:
                have[bare[0] // 4] = have.get(bare[0] // 4, 0) + len(bare)
                if have[bare[0] // 4] == 4:
                    toq.append(bare[0] // 4)

        accs = {}

        def row_ops(r):
            chains = row_chains(r, LONG.get(r, LONGEST))
            accs[r] = []
            ops = []

            def first(c):
                dx, dy, n = c[0]
                acc = apool.tile([P, C], F32, name="acc", tag="acc")
                accs[r].append((dx, acc))
                nc.scalar.activation(out=acc[:], in_=vrows[r + dy][:], func=ACT.Copy, scale=scalar_of(r, n))

            def more(k, step):
                dx, dy, n = chains[k][step]
                acc = accs[r][k][1]
                nc.vector.scalar_tensor_tensor(
                    out=acc[:], in0=vrows[r + dy][:], scalar=scalar_of(r, n), in1=acc[:], op0=ALU.mult, op1=ALU.add
                )

            firsts = [(r + c[0][1], lambda c=c: first(c)) for c in chains]
            rest = []
            for k0 in range(0, len(chains), 2):
                for step in range(1, 7):
                    for k in (k0, k0 + 1):
                        if k < len(chains) and step < len(chains[k]):
                            rest.append((k, r + chains[k][step][1], lambda k=k, step=step: more(k, step)))
            n = 0
            for k, src, f in rest:
                while n < min(len(firsts), k + LEAD):
                    ops.append(firsts[n])
                    n += 1
                ops.append((src, f))
            return ops + firsts[n:]

        def scalar_of(r, n):
            return wc2[:, r : r + 1] if n == -1 else wgt[:, r, n : n + 1]

        banks = {}

        def row_sum(r):
            if not accs[r]:
                return
            bank = psr.tile([P, 4, P], F32, name="bank", tag="row")
            todo = accs[r]
            for t in range(4):
                for k, (dx, acc) in enumerate(todo):
                    nc.tensor.matmul(
                        out=bank[:, t, :], lhsT=acc[:, P * t : P * (t + 1)], rhs=ext[:, 4 + dx : 4 + dx + P],
                        start=(k == 0), stop=(k == len(todo) - 1), is_transpose=True,
                    )
            banks[r] = bank

        def row_out(r):
            cg = context_tile(r // 4)
            y = r // CHUNK
            if r not in KEPT:
                nc.scalar.copy(out=cg[:, r % 4, :, :], in_=banks[r][:].rearrange("p t n -> p n t"))
            else:
                side = banded[y][:, :, r - KEPT_CHUNKS[y][0], :].rearrange("p t n -> p n t")
                nc.vector.tensor_tensor(
                    out=cg[:, r % 4, :, :], in0=banks[r][:].rearrange("p t n -> p n t"), in1=side, op=ALU.add
                )
            have[r // 4] = have.get(r // 4, 0) + 1

        cqs = {}

        def finish_quantize(k):
            cq = cpool.tile([P, 4 * P], U32, name="cq", tag="cq", align_bytes=64)
            cs = cpool.tile([P, 4 * P], U8, name="cs", tag="cs", align_bytes=64)
            nc.vector.quantize_mx(
                out=cq[:].bitcast(FP8X4), scales=cs[:], in_=ctxs[k][:].rearrange("p r n t -> p (r n t)")
            )
            cqs[k] = (cq, cs)

        def finish(k, gs):
            cq, cs = cqs[k]
            for g in gs:
                po = psv.tile([P, 4, B, W], F32, name="po", tag="v")
                nc.tensor.matmul_mx(
                    out=po[:].rearrange("p r b c -> p (r b c)"),
                    lhsT=wq[:, P * g : P * (g + 1)].bitcast(FP8X4), lhsT_scale=wqs[:, P * g : P * (g + 1)],
                    rhs=cq[:].bitcast(FP8X4), rhs_scale=cs[:], start=True, stop=True,
                )
                pos[k, g] = po

        def finish_store(k, gs):
            for g in gs:
                ot = (vpp if (k, g) in VOUT else opool).tile([P, B, 4, W], F32, name="ot", tag="vp" if (k, g) in VOUT else "ot")
                if (k, g) in VOUT:
                    nc.vector.tensor_scalar(
                        out=ot[:].rearrange("p b r c -> p r b c"), in0=pos[k, g][:],
                        scalar1=wbias[:, g : g + 1], scalar2=None, op0=ALU.add,
                    )
                else:
                    nc.scalar.activation(
                        out=ot[:].rearrange("p b r c -> p r b c"), in_=pos[k, g][:], func=ACT.Identity,
                        bias=wbias[:, g : g + 1],
                    )
                nc.sync.dma_start(
                    out=out[:, P * g : P * (g + 1), 4 * k : 4 * k + 4, :].rearrange("b o r c -> o b (r c)"),
                    in_=ot[:].rearrange("p b r c -> p b (r c)"),
                )

        quantize_x(0)
        at_d = {0: make_d(0)}
        make_patches(0)
        widen_x(1)
        vbias = const.tile([P, 4, P], F32, name="vbias")
        nc.vector.tensor_copy(out=vbias[:], in_=vb16[:].rearrange("p (m t) -> p t m", t=4))
        vbias2 = vbias[:].rearrange("p t m -> p (t m)")
        make_vrow(3)
        make_vrow(4)
        make_vrow(5)
        interleave_x(1)
        for r in (3, 4, 5):
            evac_vrow(r)
        make_vrow(6)
        make_vrow(7)
        evac_vrow(6)
        evac_vrow(7)
        quantize_x(1)
        wq, wqs = make_weight(ww, "wq")
        load_x(2)
        load_x(3)
        first_slot = [min(s for s in range(len(SLOTS)) if SLOTS[s][0] == y) for y in range(NCH)] + [len(SLOTS)]

        def flatten(rows):
            flat = []
            for r in rows:
                for src, f in row_ops(r):
                    flat.append((f, r, src))
                flat.append((None, r, 0))
            return flat

        heavy = flatten(HEAVY)
        light = [flatten(rows) for rows in LIGHT]
        queue = []
        for s in range(len(SLOTS) + 4):
            here = [heavy[len(heavy) * s // HSLOTS : len(heavy) * (s + 1) // HSLOTS]]
            for y in range(NCH + 1):
                k = s - first_slot[y] + EARLY[y]
                n = LSLOTS if y < NCH else TAIL
                if 0 <= k < n:
                    here.append(light[y][len(light[y]) * k // n : len(light[y]) * (k + 1) // n])
            mixed = []
            for m in range(max(len(h) for h in here)):
                mixed += [h[m] for h in here if m < len(h)]
            queue.append(mixed)
        upto = [max([12] + [src for q in queue[: s + 1 + AHEAD] for f, r, src in q]) for s in range(len(queue))]
        for r in range(8, 11):
            make_vrow(r)
        for r in range(8, 11):
            evac_vrow(r)
        make_a(0, at_d[0])
        at_d[1] = make_d(1)
        for s in range(2):
            group_values(s)
            group_evac(s, 0)
            group_evac(s, 1)
        for r in range(11, 13):
            make_vrow(r)
            evac_vrow(r)
        vdone = 13
        pb = psr.tile([P, P], BF16, name="pb", tag="row")
        nc.tensor.transpose(pb[:], wb16[:], ident16[:])
        wbias = const.tile([P, 4], F32, name="wbias")
        nc.vector.tensor_copy(out=wbias[:], in_=pb[:, 0:4])
        tosum = []
        summed = []
        tofin = []
        n_slots = len(SLOTS)
        ready = []
        for s in range(n_slots + 12):
            y = SLOTS[s][0] if s < n_slots else NCH
            k = s - first_slot[y]
            ops = queue[s] if s < len(queue) else []
            third = -(-len(ops) // 3)
            nxt = []

            def run(part):
                for f, r, src in ops[part * third : (part + 1) * third]:
                    if f is not None:
                        f()
                    else:
                        nxt.append(r)

            if s < n_slots:
                if y >= 1 and y + 1 < NCH and k == DAT[y]:
                    at_d[y + 1] = make_d(y + 1)
                for j, at_slot in XAT:
                    if s == at_slot:
                        widen_x(j)
                    if s == at_slot + 1:
                        interleave_x(j)
                    if s == at_slot + 2:
                        quantize_x(j)
                if y + 1 < NCH and k == PAT[y]:
                    make_patches(y + 1)
                if y + 1 < NCH and k == PAT[y] + 1:
                    make_a(y + 1, at_d[y + 1])
            new = []
            if s + 2 < n_slots:
                group_values(s + 2)
            while s < n_slots and vdone <= upto[s]:
                make_vrow(vdone)
                new.append(vdone)
                vdone += 1
            n_fin = 1 if s < n_slots else 2
            fin = ready[0:n_fin]
            ready = ready[n_fin:] + tofin
            tofin = []
            for g, gs in fin:
                finish(g, gs)
            if s < n_slots:
                group_banded(s)
            outs = summed
            summed = tosum[0:MAXSUM]
            tosum = tosum[MAXSUM:]
            for r in summed:
                row_sum(r)
            run(0)
            if s + 2 < n_slots:
                group_evac(s + 2, 0)
            run(1)
            if s + 2 < n_slots:
                group_evac(s + 2, 1)
            for r in new:
                evac_vrow(r)
            run(2)
            for g, gs in fin:
                finish_store(g, gs)
            if s < n_slots:
                group_copy(s)
            now = [g for g in toq]
            toq.clear()
            for g in now:
                finish_quantize(g)
                tofin.append((g, (0, 1)))
                tofin.append((g, (2, 3)))
            for r in outs:
                row_out(r)
                if have[r // 4] == 4:
                    toq.append(r // 4)
            tosum = tosum + nxt
